import numpy as np
import ml_dtypes

BF16 = ml_dtypes.bfloat16


def bf(x):
    return np.asarray(x, np.float32).astype(BF16)


def f32(x):
    return np.asarray(x, np.float32)


def f64(x):
    return np.asarray(x).astype(np.float64)


def striped(idx):
    return np.tile(idx.reshape(-1, 16).T, (8, 1))


D, S, M, DEG, N, H, K = 128, 1024, 256, 4, 4096, 512, 8


def setup_inputs():
    x = bf(np.random.standard_normal((D, S)))
    w_self = bf(np.random.standard_normal((D, M)) / np.sqrt(D))
    w_neigh = bf(np.random.standard_normal((D, M)) / np.sqrt(D * DEG))
    b = f32(0.1 * np.random.standard_normal((M, 1)))
    idx = np.concatenate([np.random.permutation(S)[:H] for _ in range(K)])
    return {"x": x, "w_self": w_self, "w_neigh": w_neigh, "b": b, "offs": striped(idx)}


def reference(x, w_self, w_neigh, b, offs):
    idx = offs[:16].T.reshape(-1)
    xs = f64(x)
    agg = xs[:, idx].reshape(D, DEG, S).sum(axis=1)
    return np.maximum(f64(w_self).T @ xs + f64(w_neigh).T @ agg + f64(b), 0.0)

@@ -1,0 +1,69 @@
+import concourse.mybir as mybir
+
+BF16, F32, U16 = mybir.dt.bfloat16, mybir.dt.float32, mybir.dt.uint16
+ADD, MAX = mybir.AluOpType.add, mybir.AluOpType.max
+
+P = 128
+NODES = 1024
+FEATURES_OUT = 256
+DEGREE = 4
+PIECE = 512
+BLOCKS = FEATURES_OUT // P
+HALVES = NODES // PIECE
+PIECE_COLS = PIECE // 16
+
+FLOPS = 2 * P * FEATURES_OUT * NODES * (1 + DEGREE)
+
+
+def tile_gresnet_kernel(tc, x, w_self, w_neigh, b, offs, out):
+    nc = tc.nc
+    with (
+        tc.tile_pool(name="held", bufs=1) as held,
+        tc.tile_pool(name="staging", bufs=BLOCKS * HALVES) as staging,
+        tc.psum_pool(name="psum", bufs=1) as psum,
+    ):
+        table = held.tile([P, NODES], BF16, name="table")
+        own_weights = held.tile([P, FEATURES_OUT], BF16, name="own_weights")
+        neigh_weights = held.tile([P, FEATURES_OUT], BF16, name="neigh_weights")
+        offsets = held.tile([P, DEGREE * NODES // 16], U16, name="offsets")
+        nc.sync.dma_start(table[:], x)
+        nc.scalar.dma_start(own_weights[:], w_self)
+        nc.sync.dma_start(offsets[:], offs)
+        nc.scalar.dma_start(neigh_weights[:], w_neigh)
+        bias = [held.tile([P, 1], F32, name=f"bias{t}") for t in range(BLOCKS)]
+        for t in range(BLOCKS):
+            nc.gpsimd.dma_start(bias[t][:], b[t * P : (t + 1) * P, :])
+
+        banks = {
+            (t, h): psum.tile([P, PIECE], F32, name=f"bank{t}{h}")
+            for t in range(BLOCKS)
+            for h in range(HALVES)
+        }
+
+        for (t, h), bank in banks.items():
+            nc.tensor.matmul(
+                bank[:],
+                own_weights[:, t * P : (t + 1) * P],
+                table[:, h * PIECE : (h + 1) * PIECE],
+                start=True,
+                stop=False,
+            )
+
+        for (t, h), bank in banks.items():
+            for e in range(DEGREE):
+                piece = e * HALVES + h
+                neighbours = table[:].indirect(
+                    offsets[:, piece * PIECE_COLS : (piece + 1) * PIECE_COLS]
+                )
+                nc.tensor.matmul(
+                    bank[:],
+                    neigh_weights[:, t * P : (t + 1) * P],
+                    neighbours,
+                    start=False,
+                    stop=(e == DEGREE - 1),
+                )
+            result = staging.tile([P, PIECE], F32, name="result")
+            nc.vector.tensor_scalar(result[:], bank[:], bias[t][:], 0.0, ADD, MAX)
+            nc.sync.dma_start(
+                out[t * P : (t + 1) * P, h * PIECE : (h + 1) * PIECE], result[:]
+            )

@@ -11,6 +11,7 @@ PIECE = 512
 BLOCKS = FEATURES_OUT // P
 HALVES = NODES // PIECE
 PIECE_COLS = PIECE // 16
+WARM_UP = 16
 
 FLOPS = 2 * P * FEATURES_OUT * NODES * (1 + DEGREE)
 
@@ -32,7 +33,13 @@ def tile_gresnet_kernel(tc, x, w_self, w_neigh, b, offs, out):
         nc.scalar.dma_start(neigh_weights[:], w_neigh)
         bias = [held.tile([P, 1], F32, name=f"bias{t}") for t in range(BLOCKS)]
         for t in range(BLOCKS):
-            nc.gpsimd.dma_start(bias[t][:], b[t * P : (t + 1) * P, :])
+            nc.scalar.dma_start(bias[t][:], b[t * P : (t + 1) * P, :])
+
+        zeros = held.tile([P, P], BF16, name="zeros")
+        nc.gpsimd.memset(zeros[:], 0.0)
+        unread = psum.tile([P, P], F32, name="unread")
+        for i in range(WARM_UP):
+            nc.tensor.matmul(unread[:], zeros[:], zeros[:], start=True, stop=True)
 
         banks = {
             (t, h): psum.tile([P, PIECE], F32, name=f"bank{t}{h}")

@@ -11,6 +11,7 @@ PIECE = 512
 BLOCKS = FEATURES_OUT // P
 HALVES = NODES // PIECE
 PIECE_COLS = PIECE // 16
+PART = PIECE // 2
 WARM_UP = 16
 
 FLOPS = 2 * P * FEATURES_OUT * NODES * (1 + DEGREE)
@@ -20,7 +21,7 @@ def tile_gresnet_kernel(tc, x, w_self, w_neigh, b, offs, out):
     nc = tc.nc
     with (
         tc.tile_pool(name="held", bufs=1) as held,
-        tc.tile_pool(name="staging", bufs=BLOCKS * HALVES) as staging,
+        tc.tile_pool(name="staging", bufs=2 * BLOCKS * HALVES) as staging,
         tc.psum_pool(name="psum", bufs=1) as psum,
     ):
         table = held.tile([P, NODES], BF16, name="table")
@@ -69,8 +70,10 @@ def tile_gresnet_kernel(tc, x, w_self, w_neigh, b, offs, out):
                     start=False,
                     stop=(e == DEGREE - 1),
                 )
-            result = staging.tile([P, PIECE], F32, name="result")
-            nc.vector.tensor_scalar(result[:], bank[:], bias[t][:], 0.0, ADD, MAX)
-            nc.sync.dma_start(
-                out[t * P : (t + 1) * P, h * PIECE : (h + 1) * PIECE], result[:]
-            )
+            for part, queue in enumerate((nc.sync, nc.scalar)):
+                result = staging.tile([P, PART], F32, name="result")
+                nc.vector.tensor_scalar(
+                    result[:], bank[:, part * PART : (part + 1) * PART], bias[t][:], 0.0, ADD, MAX
+                )
+                first = h * PIECE + part * PART
+                queue.dma_start(out[t * P : (t + 1) * P, first : first + PART], result[:])

@@ -12,7 +12,7 @@ BLOCKS = FEATURES_OUT // P
 HALVES = NODES // PIECE
 PIECE_COLS = PIECE // 16
 PART = PIECE // 2
-WARM_UP = 16
+WARM_UP = 12
 
 FLOPS = 2 * P * FEATURES_OUT * NODES * (1 + DEGREE)
 

@@ -37,7 +37,7 @@ def tile_gresnet_kernel(tc, x, w_self, w_neigh, b, offs, out):
             nc.scalar.dma_start(bias[t][:], b[t * P : (t + 1) * P, :])
 
         zeros = held.tile([P, P], BF16, name="zeros")
-        nc.gpsimd.memset(zeros[:], 0.0)
+        nc.vector.memset(zeros[:], 0.0)
         unread = psum.tile([P, P], F32, name="unread")
         for i in range(WARM_UP):
             nc.tensor.matmul(unread[:], zeros[:], zeros[:], start=True, stop=True)

import concourse.mybir as mybir

BF16, F32, U16 = mybir.dt.bfloat16, mybir.dt.float32, mybir.dt.uint16
ADD, MAX = mybir.AluOpType.add, mybir.AluOpType.max

P = 128
NODES = 1024
FEATURES_OUT = 256
DEGREE = 4
PIECE = 512
BLOCKS = FEATURES_OUT // P
HALVES = NODES // PIECE
PIECE_COLS = PIECE // 16
PART = PIECE // 2
WARM_UP = 12

FLOPS = 2 * P * FEATURES_OUT * NODES * (1 + DEGREE)


def tile_gresnet_kernel(tc, x, w_self, w_neigh, b, offs, out):
    nc = tc.nc
    with (
        tc.tile_pool(name="held", bufs=1) as held,
        tc.tile_pool(name="staging", bufs=2 * BLOCKS * HALVES) as staging,
        tc.psum_pool(name="psum", bufs=1) as psum,
    ):
        table = held.tile([P, NODES], BF16, name="table")
        own_weights = held.tile([P, FEATURES_OUT], BF16, name="own_weights")
        neigh_weights = held.tile([P, FEATURES_OUT], BF16, name="neigh_weights")
        offsets = held.tile([P, DEGREE * NODES // 16], U16, name="offsets")
        nc.sync.dma_start(table[:], x)
        nc.scalar.dma_start(own_weights[:], w_self)
        nc.sync.dma_start(offsets[:], offs)
        nc.scalar.dma_start(neigh_weights[:], w_neigh)
        bias = [held.tile([P, 1], F32, name=f"bias{t}") for t in range(BLOCKS)]
        for t in range(BLOCKS):
            nc.scalar.dma_start(bias[t][:], b[t * P : (t + 1) * P, :])

        zeros = held.tile([P, P], BF16, name="zeros")
        nc.vector.memset(zeros[:], 0.0)
        unread = psum.tile([P, P], F32, name="unread")
        for i in range(WARM_UP):
            nc.tensor.matmul(unread[:], zeros[:], zeros[:], start=True, stop=True)

        banks = {
            (t, h): psum.tile([P, PIECE], F32, name=f"bank{t}{h}")
            for t in range(BLOCKS)
            for h in range(HALVES)
        }

        for (t, h), bank in banks.items():
            nc.tensor.matmul(
                bank[:],
                own_weights[:, t * P : (t + 1) * P],
                table[:, h * PIECE : (h + 1) * PIECE],
                start=True,
                stop=False,
            )

        for (t, h), bank in banks.items():
            for e in range(DEGREE):
                piece = e * HALVES + h
                neighbours = table[:].indirect(
                    offsets[:, piece * PIECE_COLS : (piece + 1) * PIECE_COLS]
                )
                nc.tensor.matmul(
                    bank[:],
                    neigh_weights[:, t * P : (t + 1) * P],
                    neighbours,
                    start=False,
                    stop=(e == DEGREE - 1),
                )
            for part, queue in enumerate((nc.sync, nc.scalar)):
                result = staging.tile([P, PART], F32, name="result")
                nc.vector.tensor_scalar(
                    result[:], bank[:, part * PART : (part + 1) * PART], bias[t][:], 0.0, ADD, MAX
                )
                first = h * PIECE + part * PART
                queue.dma_start(out[t * P : (t + 1) * P, first : first + PART], result[:])
